import numpy as np
import ml_dtypes


def mxq(x, axis, fmt="e4m3"):
    dtype, down = {"e4m3": (ml_dtypes.float8_e4m3fn, 7), "e5m2": (ml_dtypes.float8_e5m2, 14)}[fmt]
    v = np.moveaxis(np.asarray(x, np.float32).astype(ml_dtypes.bfloat16).astype(np.float64), axis, -1)
    blocks = v.reshape(v.shape[:-1] + (-1, 32))
    amax = np.abs(blocks).max(-1, keepdims=True)
    byte = np.maximum(np.where(amax > 0, np.frexp(amax)[1] - 1 + 127, 0) - down, 1)
    scale = np.exp2(byte - 127.0)
    codes = (blocks / scale).astype(np.float32).astype(dtype).astype(np.float64)
    return np.moveaxis((codes * scale).reshape(v.shape), -1, axis)


WIDE = False


def mx_kscale(k):
    if not WIDE:
        return np.ones(k)
    levels = np.array([10, -10, 5, -5, 0])
    a = np.random.permutation(np.resize(levels, k // 512 * 4)).reshape(k // 512, 4)
    idx = np.arange(k)
    return np.exp2(a[idx // 512, idx % 128 // 32])


BF16 = ml_dtypes.bfloat16


def bf(x):
    return np.asarray(x, np.float32).astype(BF16)


def f64(x):
    return np.asarray(x).astype(np.float64)


M, N, E, P, S, B, KT = 1024, 512, 16, 32, 17, 128, 2


def setup_inputs():
    s = mx_kscale(M)
    return {
        "z": bf(np.random.standard_normal((M, B)) * s[:, None]),
        "mlp_out": bf(np.random.standard_normal((B, E)) * 0.65),
        "t2": bf(0.5 + 0.1 * np.random.random_sample(1)),
        "A": bf(np.random.standard_normal((E, M)) * 0.5 / s),
        "W": bf(np.random.standard_normal((E, M, M)) / np.sqrt(M) / s),
        "h": bf(np.random.standard_normal((E, M)) * 0.1),
    }


def reference(z, mlp_out, t2, A, W, h):
    z = f64(z)
    lg = -f64(mlp_out).T / f64(t2)[0]
    ex = np.exp(lg - lg.max(axis=0, keepdims=True))
    w_exp = ex / ex.sum(axis=0, keepdims=True)
    zcat = np.concatenate([z[:-P], np.maximum(z[-P:], 0.0)], axis=0)
    Az = f64(A)[:, :, None] * z[None, :, :]
    Wz = mxq(f64(W), 2, "e4m3") @ mxq(zcat, 0, "e4m3")
    expert_out = Az + Wz + f64(h)[:, :, None]
    return np.sum(expert_out * w_exp[:, None, :], axis=0)

@@ -1,0 +1,231 @@
+from contextlib import ExitStack
+
+import concourse.mybir as mybir
+from concourse.masks import make_identity
+
+F32 = mybir.dt.float32
+BF16 = mybir.dt.bfloat16
+I32 = mybir.dt.int32
+U32 = mybir.dt.uint32
+U8 = mybir.dt.uint8
+FP8X4 = mybir.dt.float8_e4m3fn_x4
+ALU = mybir.AluOpType
+ACT = mybir.ActivationFunctionType
+AX = mybir.AxisListType
+
+P = 128
+M = 1024
+E = 16
+B = 128
+FLOPS = 2 * E * M * M * B + 4 * E * M * B
+
+PIN = False
+W_BUFS = 6
+V_EVERY = 16
+NU = 2 * E
+
+
+def tile_dynamix_pb_kernel(tc, z, mlp_out, t2, A, W, h, out):
+    nc = tc.nc
+    with ExitStack() as ctx:
+        const = ctx.enter_context(tc.tile_pool(name="const", bufs=1))
+        wpool = ctx.enter_context(tc.tile_pool(name="wpool", bufs=W_BUFS))
+        gpool = ctx.enter_context(tc.tile_pool(name="gpool", bufs=3))
+        qpool = ctx.enter_context(tc.tile_pool(name="qpool", bufs=3))
+        opool = ctx.enter_context(tc.tile_pool(name="opool", bufs=2))
+        pt = ctx.enter_context(tc.psum_pool(name="pt", bufs=6))
+        pm = ctx.enter_context(tc.psum_pool(name="pm", bufs=2))
+        if PIN:
+            ctx.enter_context(tc.manual_schedule())
+
+        w_tiles = {}
+
+        def load_w(e, pieces):
+            wt = wpool.tile([P, 8 * M], BF16, name="wt", tag="wt")
+            src = W[e].rearrange("(p t) k -> p (t k)", t=8)
+            step = 8 * M // pieces
+            for c in range(pieces):
+                nc.sync.dma_start(out=wt[:, c * step:(c + 1) * step], in_=src[:, c * step:(c + 1) * step])
+            w_tiles[e] = wt
+
+        def pieces_of(e):
+            return 4 if e in (0, E - 1) else 1
+
+        for e in range(W_BUFS):
+            load_w(e, pieces_of(e))
+
+        mlp = const.tile([P, E], BF16, name="mlp")
+        nc.scalar.dma_start(out=mlp[:], in_=mlp_out)
+        t2b = const.tile([P, 1], BF16, name="t2b")
+        nc.scalar.dma_start(out=t2b[:], in_=t2.partition_broadcast(P))
+        zq = const.tile([P, 8 * B], BF16, name="zq")
+        nc.scalar.dma_start(
+            out=zq[:].rearrange("p (c x) -> p c x", c=4),
+            in_=z.rearrange("(c p e) b -> p c (e b)", c=4, p=P, e=2),
+        )
+        ah = const.tile([P, 2 * M], BF16, name="ah")
+        nc.vector.memset(ah[:].bitcast(I32), 0)
+        for s in range(3):
+            nc.scalar.dma_start(out=ah[16 * s:16 * s + 16, 0:M], in_=A)
+            nc.scalar.dma_start(out=ah[16 * s:16 * s + 16, M:2 * M], in_=h)
+        zm = const.tile([P, 8 * B], BF16, name="zm")
+        nc.scalar.dma_start(out=zm[:], in_=z.rearrange("(p t) b -> p (t b)", t=8))
+
+        ident_f = const.tile([P, P], F32, name="ident_f")
+        make_identity(nc, ident_f[:])
+        ident_b = const.tile([P, P], BF16, name="ident_b")
+        make_identity(nc, ident_b[:])
+        warm = const.tile([P, 1], F32, name="warm")
+        nc.vector.memset(warm[:], 0.0)
+        warm2 = const.tile([P, 1], F32, name="warm2")
+        nc.scalar.activation(out=warm2[:], in_=warm[:], func=ACT.Exp)
+        acc = const.tile([P, M], F32, name="acc")
+        nc.vector.memset(acc[:], 0.0)
+        xs = const.tile([P, P], BF16, name="xs")
+        nc.vector.memset(xs[:].bitcast(I32), 0)
+
+        mask = const.tile([P, 1], F32, name="mask")
+        nc.vector.tensor_reduce(out=mask[:], in_=ident_f[:, 112:128], axis=AX.X, op=ALU.add)
+        floor = const.tile([P, 1], F32, name="floor")
+        nc.vector.tensor_scalar(out=floor[:], in0=mask[:], scalar1=-1.0, scalar2=3.4e38, op0=ALU.add, op1=ALU.mult)
+        nc.vector.tensor_scalar(out=zq[:, 768:1024], in0=zq[:, 768:1024], scalar1=floor[:, 0:1], scalar2=None, op0=ALU.max)
+        zg = const.tile([P, 8 * B], BF16, name="zg", align_bytes=64)
+        nc.vector.tensor_copy(
+            out=zg[:].rearrange("p (g b j) -> p g b j", g=2, j=4),
+            in_=zq[:].rearrange("p (g j b) -> p g b j", g=2, j=4),
+        )
+        zc = const.tile([P, 2 * B], U32, name="zc", align_bytes=64)
+        zs = const.tile([P, 2 * B], U8, name="zs", align_bytes=64)
+        nc.vector.quantize_mx(out=zc[:].bitcast(FP8X4), scales=zs[:], in_=zg[:])
+
+        rt = const.tile([P, 1], F32, name="rt")
+        nc.vector.reciprocal(out=rt[:], in_=t2b[:])
+        lg = const.tile([P, E], F32, name="lg")
+        nc.vector.tensor_scalar(out=lg[:], in0=mlp[:], scalar1=rt[:, 0:1], scalar2=-1.0, op0=ALU.mult, op1=ALU.mult)
+        mx = const.tile([P, 1], F32, name="mx")
+        nc.vector.tensor_reduce(out=mx[:], in_=lg[:], axis=AX.X, op=ALU.max)
+        nmx = const.tile([P, 1], F32, name="nmx")
+        nc.vector.tensor_scalar(out=nmx[:], in0=mx[:], scalar1=-1.0, scalar2=None, op0=ALU.mult)
+        ex = const.tile([P, E], F32, name="ex")
+        sm = const.tile([P, 1], F32, name="sm")
+        nc.scalar.activation(out=ex[:], in_=lg[:], func=ACT.Exp, bias=nmx[:, 0:1], scale=1.0, accum_out=sm[:])
+        rs = const.tile([P, 1], F32, name="rs")
+        nc.vector.reciprocal(out=rs[:], in_=sm[:])
+        wg = const.tile([P, E], F32, name="wg")
+        nc.vector.tensor_scalar(out=wg[:], in0=ex[:], scalar1=rs[:, 0:1], scalar2=None, op0=ALU.mult)
+
+        nc.vector.tensor_copy(out=xs[:, 0:16], in_=wg[:])
+        r1 = const.tile([P, E], F32, name="r1")
+        nc.vector.tensor_tensor(out=r1[:], in0=wg[:], in1=xs[:, 0:16], op=ALU.subtract)
+        nc.vector.tensor_copy(out=xs[:, 16:32], in_=r1[:])
+        r2 = const.tile([P, E], F32, name="r2")
+        nc.vector.tensor_tensor(out=r2[:], in0=r1[:], in1=xs[:, 16:32], op=ALU.subtract)
+        nc.vector.tensor_copy(out=xs[:, 32:48], in_=r2[:])
+
+        aht = const.tile([P, 2 * M], BF16, name="aht")
+        nc.gpsimd.tensor_scalar(
+            out=aht[:].rearrange("k (a t p) -> k a t p", a=2, t=8),
+            in0=ah[:].rearrange("k (a p t) -> k a t p", a=2, t=8),
+            scalar1=1.0, scalar2=0.0, op0=ALU.mult, op1=ALU.add,
+        )
+        rw = const.tile([P, B], BF16, name="rw")
+        base = const.tile([P, M], F32, name="base")
+
+        def gate_transpose():
+            xp = pt.tile([P, P], BF16, name="xp", tag="tp")
+            nc.tensor.transpose(xp[:], xs[:], ident_b[:])
+            nc.vector.tensor_copy(out=rw[:], in_=xp[:])
+
+        def base_step(a, hb):
+            gb = pt.tile([P, 512], F32, name="gb", tag="tp")
+            for tl in range(4):
+                col = (a * 8 + 4 * hb + tl) * P
+                nc.tensor.matmul(gb[:, tl * P:(tl + 1) * P], lhsT=aht[:, col:col + P], rhs=rw[:], start=True, stop=True)
+            sl = slice(hb * 512, (hb + 1) * 512)
+            if a == 0:
+                nc.vector.tensor_tensor(out=base[:, sl], in0=gb[:], in1=zm[:, sl], op=ALU.mult)
+            else:
+                nc.vector.tensor_tensor(out=base[:, sl], in0=gb[:], in1=base[:, sl], op=ALU.add)
+
+        g_tiles = {}
+        q_tiles = {}
+        m_tiles = {}
+
+        def stage_a(i):
+            e, hh = divmod(i, 2)
+            w32 = w_tiles[e][:].bitcast(F32)
+            gt = gpool.tile([P, 4096], BF16, name="gt", tag="gt", align_bytes=64)
+            g32 = gt[:].bitcast(F32)
+            for j in range(4):
+                g, tp = divmod(j, 2)
+                bank = pt.tile([P, 512], F32, name="bank", tag="tp")
+                for u in range(2):
+                    for t_ in range(2):
+                        t = 4 * hh + 2 * tp + t_
+                        col = t * 512 + (2 * g + u) * P
+                        pos = (2 * u + t_) * P
+                        nc.tensor.transpose(bank[:, pos:pos + P], w32[:, col:col + P], ident_f[:])
+                dst = g32[:, g * 1024 + tp * 512:g * 1024 + (tp + 1) * 512].rearrange("p (c u) -> p c u", u=2)
+                srcv = bank[:].rearrange("p (u c) -> p c u", u=2)
+                if (4 * i + j) % V_EVERY == V_EVERY - 1:
+                    nc.vector.tensor_copy(out=dst, in_=srcv)
+                else:
+                    nc.scalar.copy(out=dst, in_=srcv)
+            g_tiles[i] = gt
+
+        def stage_b(i):
+            cw = qpool.tile([P, 1024], U32, name="cw", tag="cw", align_bytes=64)
+            cs = qpool.tile([P, 1024], U8, name="cs", tag="cs", align_bytes=64)
+            nc.vector.quantize_mx(out=cw[:].bitcast(FP8X4), scales=cs[:], in_=g_tiles[i][:])
+            q_tiles[i] = (cw, cs)
+
+        def stage_c(i):
+            cw, cs = q_tiles[i]
+            ps = pm.tile([P, 512], F32, name="ps", tag="ps")
+            for g in range(2):
+                nc.tensor.matmul_mx(
+                    out=ps[:],
+                    lhsT=zc[:, g * B:(g + 1) * B].bitcast(FP8X4),
+                    lhsT_scale=zs[:, g * B:(g + 1) * B],
+                    rhs=cw[:, g * 512:(g + 1) * 512].bitcast(FP8X4),
+                    rhs_scale=cs[:, g * 512:(g + 1) * 512],
+                    start=(g == 0),
+                    stop=(g == 1),
+                )
+            m_tiles[i] = ps
+
+        def stage_d(i):
+            e, hh = divmod(i, 2)
+            sl = slice(hh * 512, (hh + 1) * 512)
+            nc.vector.scalar_tensor_tensor(
+                out=acc[:, sl], in0=m_tiles[i][:], scalar=wg[:, e:e + 1], in1=acc[:, sl], op0=ALU.mult, op1=ALU.add
+            )
+
+        def finish(hh):
+            fb = pt.tile([P, 512], F32, name="fb", tag="tp")
+            for tl in range(4):
+                col = (4 * hh + tl) * P
+                nc.tensor.transpose(fb[:, tl * P:(tl + 1) * P], acc[:, col:col + P], ident_f[:])
+            fin = opool.tile([P, 512], F32, name="fin", tag="fin")
+            sl = slice(hh * 512, (hh + 1) * 512)
+            nc.vector.tensor_tensor(out=fin[:], in0=fb[:], in1=base[:, sl], op=ALU.add)
+            nc.sync.dma_start(out=out.rearrange("(p t) b -> p (t b)", t=8)[:, sl], in_=fin[:])
+
+        extra = {4: lambda: gate_transpose(), 5: lambda: base_step(0, 0), 6: lambda: base_step(1, 0),
+                 7: lambda: base_step(0, 1), 8: lambda: base_step(1, 1)}
+
+        for i in range(NU + 3):
+            if i < NU:
+                stage_a(i)
+                if i % 2 == 1 and i // 2 + W_BUFS < E:
+                    load_w(i // 2 + W_BUFS, pieces_of(i // 2 + W_BUFS))
+            if i in extra:
+                extra[i]()
+            if 1 <= i <= NU:
+                stage_b(i - 1)
+            if 2 <= i <= NU + 1:
+                stage_c(i - 2)
+            if i >= 3:
+                stage_d(i - 3)
+                if i - 3 >= NU - 2:
+                    finish(i - 3 - (NU - 2))

@@ -19,7 +19,7 @@ E = 16
 B = 128
 FLOPS = 2 * E * M * M * B + 4 * E * M * B
 
-PIN = False
+PIN = True
 W_BUFS = 6
 V_EVERY = 16
 NU = 2 * E

@@ -19,84 +19,95 @@ E = 16
 B = 128
 FLOPS = 2 * E * M * M * B + 4 * E * M * B
 
-PIN = True
-W_BUFS = 6
-V_EVERY = 16
-NU = 2 * E
+PIN = False
+W_BUFS = 12
+TP_BUFS = 6
+V_PERIOD = 4
+
+
+def make_units():
+    units = []
+    for e in range(E - 2):
+        units.append((e, 0, 4))
+        units.append((e, 4, 4))
+    units.extend([(E - 2, 0, 4), (E - 1, 0, 4), (E - 2, 4, 4), (E - 1, 4, 2), (E - 1, 6, 2)])
+    return units
 
 
 def tile_dynamix_pb_kernel(tc, z, mlp_out, t2, A, W, h, out):
     nc = tc.nc
+    units = make_units()
+    nu = len(units)
+    bunches = [[2 * s, 2 * s + 1] for s in range(15)] + [[30, 31, 32]]
+    finish_after = {29: (0, 4), 31: (4, 2), 32: (6, 2)}
     with ExitStack() as ctx:
         const = ctx.enter_context(tc.tile_pool(name="const", bufs=1))
         wpool = ctx.enter_context(tc.tile_pool(name="wpool", bufs=W_BUFS))
         gpool = ctx.enter_context(tc.tile_pool(name="gpool", bufs=3))
         qpool = ctx.enter_context(tc.tile_pool(name="qpool", bufs=3))
         opool = ctx.enter_context(tc.tile_pool(name="opool", bufs=2))
-        pt = ctx.enter_context(tc.psum_pool(name="pt", bufs=6))
-        pm = ctx.enter_context(tc.psum_pool(name="pm", bufs=2))
+        pt = ctx.enter_context(tc.psum_pool(name="pt", bufs=TP_BUFS))
+        pm = ctx.enter_context(tc.psum_pool(name="pm", bufs=8 - TP_BUFS))
         if PIN:
             ctx.enter_context(tc.manual_schedule())
 
         w_tiles = {}
 
-        def load_w(e, pieces):
-            wt = wpool.tile([P, 8 * M], BF16, name="wt", tag="wt")
+        def load_w(i, pieces=1):
+            e, t0, nt = units[i]
+            wt = wpool.tile([P, 4 * M], BF16, name="wt", tag="wt")
             src = W[e].rearrange("(p t) k -> p (t k)", t=8)
-            step = 8 * M // pieces
+            step = nt * M // pieces
             for c in range(pieces):
-                nc.sync.dma_start(out=wt[:, c * step:(c + 1) * step], in_=src[:, c * step:(c + 1) * step])
-            w_tiles[e] = wt
+                nc.sync.dma_start(
+                    out=wt[:, c * step:(c + 1) * step], in_=src[:, t0 * M + c * step:t0 * M + (c + 1) * step]
+                )
+            w_tiles[i] = wt
 
-        def pieces_of(e):
-            return 4 if e in (0, E - 1) else 1
-
-        for e in range(W_BUFS):
-            load_w(e, pieces_of(e))
+        warm = const.tile([P, 1], F32, name="warm")
+        nc.vector.memset(warm[:], 0.0)
+        ah = const.tile([P, 2 * M], BF16, name="ah")
+        nc.vector.memset(ah[:].bitcast(I32), 0)
+        xs = const.tile([P, P], BF16, name="xs")
+        nc.vector.memset(xs[:].bitcast(I32), 0)
+        warm2 = const.tile([P, 1], F32, name="warm2")
+        nc.scalar.activation(out=warm2[:], in_=warm[:], func=ACT.Exp)
 
         mlp = const.tile([P, E], BF16, name="mlp")
-        nc.scalar.dma_start(out=mlp[:], in_=mlp_out)
+        nc.sync.dma_start(out=mlp[:], in_=mlp_out)
         t2b = const.tile([P, 1], BF16, name="t2b")
-        nc.scalar.dma_start(out=t2b[:], in_=t2.partition_broadcast(P))
+        nc.sync.dma_start(out=t2b[:], in_=t2.partition_broadcast(P))
+        load_w(0, pieces=2)
         zq = const.tile([P, 8 * B], BF16, name="zq")
-        nc.scalar.dma_start(
+        nc.sync.dma_start(
             out=zq[:].rearrange("p (c x) -> p c x", c=4),
             in_=z.rearrange("(c p e) b -> p c (e b)", c=4, p=P, e=2),
         )
-        ah = const.tile([P, 2 * M], BF16, name="ah")
-        nc.vector.memset(ah[:].bitcast(I32), 0)
+        for i in range(1, 4):
+            load_w(i)
         for s in range(3):
-            nc.scalar.dma_start(out=ah[16 * s:16 * s + 16, 0:M], in_=A)
-            nc.scalar.dma_start(out=ah[16 * s:16 * s + 16, M:2 * M], in_=h)
+            nc.sync.dma_start(out=ah[16 * s:16 * s + 16, 0:M], in_=A)
+            nc.sync.dma_start(out=ah[16 * s:16 * s + 16, M:2 * M], in_=h)
         zm = const.tile([P, 8 * B], BF16, name="zm")
-        nc.scalar.dma_start(out=zm[:], in_=z.rearrange("(p t) b -> p (t b)", t=8))
+        nc.sync.dma_start(out=zm[:], in_=z.rearrange("(p t) b -> p (t b)", t=8))
+        for i in range(4, W_BUFS):
+            load_w(i)
 
         ident_f = const.tile([P, P], F32, name="ident_f")
         make_identity(nc, ident_f[:])
         ident_b = const.tile([P, P], BF16, name="ident_b")
         make_identity(nc, ident_b[:])
-        warm = const.tile([P, 1], F32, name="warm")
-        nc.vector.memset(warm[:], 0.0)
-        warm2 = const.tile([P, 1], F32, name="warm2")
-        nc.scalar.activation(out=warm2[:], in_=warm[:], func=ACT.Exp)
-        acc = const.tile([P, M], F32, name="acc")
-        nc.vector.memset(acc[:], 0.0)
-        xs = const.tile([P, P], BF16, name="xs")
-        nc.vector.memset(xs[:].bitcast(I32), 0)
+        aht = const.tile([P, 2 * M], BF16, name="aht")
+        nc.gpsimd.tensor_scalar(
+            out=aht[:].rearrange("k (a t p) -> k a t p", a=2, t=8),
+            in0=ah[:].rearrange("k (a p t) -> k a t p", a=2, t=8),
+            scalar1=1.0, scalar2=0.0, op0=ALU.mult, op1=ALU.add,
+        )
 
         mask = const.tile([P, 1], F32, name="mask")
         nc.vector.tensor_reduce(out=mask[:], in_=ident_f[:, 112:128], axis=AX.X, op=ALU.add)
         floor = const.tile([P, 1], F32, name="floor")
         nc.vector.tensor_scalar(out=floor[:], in0=mask[:], scalar1=-1.0, scalar2=3.4e38, op0=ALU.add, op1=ALU.mult)
-        nc.vector.tensor_scalar(out=zq[:, 768:1024], in0=zq[:, 768:1024], scalar1=floor[:, 0:1], scalar2=None, op0=ALU.max)
-        zg = const.tile([P, 8 * B], BF16, name="zg", align_bytes=64)
-        nc.vector.tensor_copy(
-            out=zg[:].rearrange("p (g b j) -> p g b j", g=2, j=4),
-            in_=zq[:].rearrange("p (g j b) -> p g b j", g=2, j=4),
-        )
-        zc = const.tile([P, 2 * B], U32, name="zc", align_bytes=64)
-        zs = const.tile([P, 2 * B], U8, name="zs", align_bytes=64)
-        nc.vector.quantize_mx(out=zc[:].bitcast(FP8X4), scales=zs[:], in_=zg[:])
 
         rt = const.tile([P, 1], F32, name="rt")
         nc.vector.reciprocal(out=rt[:], in_=t2b[:])
@@ -108,124 +119,173 @@ def tile_dynamix_pb_kernel(tc, z, mlp_out, t2, A, W, h, out):
         nc.vector.tensor_scalar(out=nmx[:], in0=mx[:], scalar1=-1.0, scalar2=None, op0=ALU.mult)
         ex = const.tile([P, E], F32, name="ex")
         sm = const.tile([P, 1], F32, name="sm")
-        nc.scalar.activation(out=ex[:], in_=lg[:], func=ACT.Exp, bias=nmx[:, 0:1], scale=1.0, accum_out=sm[:])
         rs = const.tile([P, 1], F32, name="rs")
-        nc.vector.reciprocal(out=rs[:], in_=sm[:])
         wg = const.tile([P, E], F32, name="wg")
-        nc.vector.tensor_scalar(out=wg[:], in0=ex[:], scalar1=rs[:, 0:1], scalar2=None, op0=ALU.mult)
-
-        nc.vector.tensor_copy(out=xs[:, 0:16], in_=wg[:])
-        r1 = const.tile([P, E], F32, name="r1")
-        nc.vector.tensor_tensor(out=r1[:], in0=wg[:], in1=xs[:, 0:16], op=ALU.subtract)
-        nc.vector.tensor_copy(out=xs[:, 16:32], in_=r1[:])
-        r2 = const.tile([P, E], F32, name="r2")
-        nc.vector.tensor_tensor(out=r2[:], in0=r1[:], in1=xs[:, 16:32], op=ALU.subtract)
-        nc.vector.tensor_copy(out=xs[:, 32:48], in_=r2[:])
-
-        aht = const.tile([P, 2 * M], BF16, name="aht")
-        nc.gpsimd.tensor_scalar(
-            out=aht[:].rearrange("k (a t p) -> k a t p", a=2, t=8),
-            in0=ah[:].rearrange("k (a p t) -> k a t p", a=2, t=8),
-            scalar1=1.0, scalar2=0.0, op0=ALU.mult, op1=ALU.add,
-        )
+        zg = const.tile([P, 8 * B], BF16, name="zg", align_bytes=64)
+        zc = const.tile([P, 2 * B], U32, name="zc", align_bytes=64)
+        zs = const.tile([P, 2 * B], U8, name="zs", align_bytes=64)
+        acc = const.tile([P, M], F32, name="acc")
         rw = const.tile([P, B], BF16, name="rw")
-        base = const.tile([P, M], F32, name="base")
+        zt = const.tile([P, M], BF16, name="zt")
 
-        def gate_transpose():
-            xp = pt.tile([P, P], BF16, name="xp", tag="tp")
-            nc.tensor.transpose(xp[:], xs[:], ident_b[:])
-            nc.vector.tensor_copy(out=rw[:], in_=xp[:])
+        def gate_exp():
+            nc.scalar.activation(out=ex[:], in_=lg[:], func=ACT.Exp, bias=nmx[:, 0:1], scale=1.0, accum_out=sm[:])
 
-        def base_step(a, hb):
-            gb = pt.tile([P, 512], F32, name="gb", tag="tp")
-            for tl in range(4):
-                col = (a * 8 + 4 * hb + tl) * P
-                nc.tensor.matmul(gb[:, tl * P:(tl + 1) * P], lhsT=aht[:, col:col + P], rhs=rw[:], start=True, stop=True)
-            sl = slice(hb * 512, (hb + 1) * 512)
-            if a == 0:
-                nc.vector.tensor_tensor(out=base[:, sl], in0=gb[:], in1=zm[:, sl], op=ALU.mult)
-            else:
-                nc.vector.tensor_tensor(out=base[:, sl], in0=gb[:], in1=base[:, sl], op=ALU.add)
+        def z_and_gate():
+            nc.vector.tensor_scalar(
+                out=zq[:, 768:1024], in0=zq[:, 768:1024], scalar1=floor[:, 0:1], scalar2=None, op0=ALU.max
+            )
+            nc.vector.tensor_copy(
+                out=zg[:].rearrange("p (g b j) -> p g b j", g=2, j=4),
+                in_=zq[:].rearrange("p (g j b) -> p g b j", g=2, j=4),
+            )
+            nc.vector.reciprocal(out=rs[:], in_=sm[:])
+            nc.vector.tensor_scalar(out=wg[:], in0=ex[:], scalar1=rs[:, 0:1], scalar2=None, op0=ALU.mult)
+            nc.vector.quantize_mx(out=zc[:].bitcast(FP8X4), scales=zs[:], in_=zg[:])
+
+        def gate_split():
+            nc.vector.tensor_copy(out=xs[:, 0:16], in_=wg[:])
+            r1 = const.tile([P, E], F32, name="r1")
+            nc.vector.tensor_tensor(out=r1[:], in0=wg[:], in1=xs[:, 0:16], op=ALU.subtract)
+            nc.vector.tensor_copy(out=xs[:, 16:32], in_=r1[:])
+            r2 = const.tile([P, E], F32, name="r2")
+            nc.vector.tensor_tensor(out=r2[:], in0=r1[:], in1=xs[:, 16:32], op=ALU.subtract)
+            nc.vector.tensor_copy(out=xs[:, 32:48], in_=r2[:])
+
+        side = {}
+
+        def side_tensor(s):
+            if s == 2:
+                xp = pt.tile([P, P], BF16, name="xp", tag="tp")
+                nc.tensor.transpose(xp[:], xs[:], ident_b[:])
+                side["xp"] = xp
+                zp = pt.tile([P, M], BF16, name="zp", tag="tp")
+                for t in range(8):
+                    nc.tensor.transpose(zp[:, t * P:(t + 1) * P], zm[:, t * P:(t + 1) * P], ident_b[:])
+                nc.scalar.copy(out=zt[:], in_=zp[:])
+            if s in (3, 4):
+                hb = s - 3
+                for a in range(2):
+                    gb = pt.tile([P, 512], F32, name="gb", tag="tp")
+                    col = (a * 8 + 4 * hb) * P
+                    nc.tensor.matmul(gb[:], lhsT=rw[:], rhs=aht[:, col:col + 512], start=True, stop=True)
+                    side[a] = gb
+
+        def side_vector(s):
+            if s == 1:
+                gate_split()
+            if s == 2:
+                nc.vector.tensor_copy(out=rw[:], in_=side["xp"][:])
+            if s in (3, 4):
+                sl = slice((s - 3) * 512, (s - 2) * 512)
+                tmp = opool.tile([P, 512], F32, name="tmp", tag="tmp")
+                nc.vector.tensor_tensor(out=tmp[:], in0=side[0][:], in1=zt[:, sl], op=ALU.mult)
+                nc.vector.tensor_tensor(out=acc[:, sl], in0=side[1][:], in1=acc[:, sl], op=ALU.add)
+                nc.vector.tensor_tensor(out=acc[:, sl], in0=acc[:, sl], in1=tmp[:], op=ALU.add)
 
         g_tiles = {}
         q_tiles = {}
         m_tiles = {}
 
-        def stage_a(i):
-            e, hh = divmod(i, 2)
-            w32 = w_tiles[e][:].bitcast(F32)
+        def transposes(i):
+            e, t0, nt = units[i]
+            w32 = w_tiles[i][:].bitcast(F32)
             gt = gpool.tile([P, 4096], BF16, name="gt", tag="gt", align_bytes=64)
             g32 = gt[:].bitcast(F32)
-            for j in range(4):
-                g, tp = divmod(j, 2)
-                bank = pt.tile([P, 512], F32, name="bank", tag="tp")
-                for u in range(2):
-                    for t_ in range(2):
-                        t = 4 * hh + 2 * tp + t_
-                        col = t * 512 + (2 * g + u) * P
-                        pos = (2 * u + t_) * P
-                        nc.tensor.transpose(bank[:, pos:pos + P], w32[:, col:col + P], ident_f[:])
-                dst = g32[:, g * 1024 + tp * 512:g * 1024 + (tp + 1) * 512].rearrange("p (c u) -> p c u", u=2)
-                srcv = bank[:].rearrange("p (u c) -> p c u", u=2)
-                if (4 * i + j) % V_EVERY == V_EVERY - 1:
-                    nc.vector.tensor_copy(out=dst, in_=srcv)
-                else:
-                    nc.scalar.copy(out=dst, in_=srcv)
+            for tp in range(nt // 2):
+                for g in range(2):
+                    bank = pt.tile([P, 512], F32, name="bank", tag="tp")
+                    for u in range(2):
+                        for t_ in range(2):
+                            col = (2 * tp + t_) * 512 + (2 * g + u) * P
+                            pos = (2 * u + t_) * P
+                            nc.tensor.transpose(bank[:, pos:pos + P], w32[:, col:col + P], ident_f[:])
+                    off = g * nt * 256 + tp * 512
+                    dst = g32[:, off:off + 512].rearrange("p (c u) -> p c u", u=2)
+                    srcv = bank[:].rearrange("p (u c) -> p c u", u=2)
+                    if i % V_PERIOD == 0 and i > 0 and nt == 4 and tp == 1 and g == 1:
+                        nc.vector.tensor_copy(out=dst, in_=srcv)
+                    else:
+                        nc.scalar.copy(out=dst, in_=srcv)
+                if i == 0 and tp == 0:
+                    gate_exp()
             g_tiles[i] = gt
 
-        def stage_b(i):
+        def quantise(i):
+            nt = units[i][2]
             cw = qpool.tile([P, 1024], U32, name="cw", tag="cw", align_bytes=64)
             cs = qpool.tile([P, 1024], U8, name="cs", tag="cs", align_bytes=64)
-            nc.vector.quantize_mx(out=cw[:].bitcast(FP8X4), scales=cs[:], in_=g_tiles[i][:])
+            nc.vector.quantize_mx(
+                out=cw[:, 0:nt * 256].bitcast(FP8X4), scales=cs[:, 0:nt * 256], in_=g_tiles[i][:, 0:nt * 1024]
+            )
             q_tiles[i] = (cw, cs)
 
-        def stage_c(i):
+        def multiply(i):
+            e, t0, nt = units[i]
             cw, cs = q_tiles[i]
-            ps = pm.tile([P, 512], F32, name="ps", tag="ps")
+            n = nt * P
+            if nt == 2 and t0 % 4 == 2:
+                ps, c0 = m_tiles[i - 1][0], 256
+            else:
+                ps = pm.tile([P, 512], F32, name="ps", tag="ps")
+                c0 = 0
             for g in range(2):
                 nc.tensor.matmul_mx(
-                    out=ps[:],
+                    out=ps[:, c0:c0 + n],
                     lhsT=zc[:, g * B:(g + 1) * B].bitcast(FP8X4),
                     lhsT_scale=zs[:, g * B:(g + 1) * B],
-                    rhs=cw[:, g * 512:(g + 1) * 512].bitcast(FP8X4),
-                    rhs_scale=cs[:, g * 512:(g + 1) * 512],
+                    rhs=cw[:, g * n:(g + 1) * n].bitcast(FP8X4),
+                    rhs_scale=cs[:, g * n:(g + 1) * n],
                     start=(g == 0),
                     stop=(g == 1),
                 )
-            m_tiles[i] = ps
+            m_tiles[i] = (ps, c0)
 
-        def stage_d(i):
-            e, hh = divmod(i, 2)
-            sl = slice(hh * 512, (hh + 1) * 512)
-            nc.vector.scalar_tensor_tensor(
-                out=acc[:, sl], in0=m_tiles[i][:], scalar=wg[:, e:e + 1], in1=acc[:, sl], op0=ALU.mult, op1=ALU.add
-            )
+        def mix(i):
+            e, t0, nt = units[i]
+            ps, c0 = m_tiles[i]
+            sl = slice(t0 * P, (t0 + nt) * P)
+            if e == 0:
+                nc.vector.tensor_scalar(
+                    out=acc[:, sl], in0=ps[:, c0:c0 + nt * P], scalar1=wg[:, 0:1], scalar2=None, op0=ALU.mult
+                )
+            else:
+                nc.vector.scalar_tensor_tensor(
+                    out=acc[:, sl], in0=ps[:, c0:c0 + nt * P], scalar=wg[:, e:e + 1], in1=acc[:, sl],
+                    op0=ALU.mult, op1=ALU.add,
+                )
 
-        def finish(hh):
+        def finish(t0, nt):
             fb = pt.tile([P, 512], F32, name="fb", tag="tp")
-            for tl in range(4):
-                col = (4 * hh + tl) * P
+            for tl in range(nt):
+                col = (t0 + tl) * P
                 nc.tensor.transpose(fb[:, tl * P:(tl + 1) * P], acc[:, col:col + P], ident_f[:])
             fin = opool.tile([P, 512], F32, name="fin", tag="fin")
-            sl = slice(hh * 512, (hh + 1) * 512)
-            nc.vector.tensor_tensor(out=fin[:], in0=fb[:], in1=base[:, sl], op=ALU.add)
-            nc.sync.dma_start(out=out.rearrange("(p t) b -> p (t b)", t=8)[:, sl], in_=fin[:])
+            nc.scalar.copy(out=fin[:, 0:nt * P], in_=fb[:, 0:nt * P])
+            nc.sync.dma_start(
+                out=out.rearrange("(p t) b -> p (t b)", t=8)[:, t0 * P:(t0 + nt) * P], in_=fin[:, 0:nt * P]
+            )
 
-        extra = {4: lambda: gate_transpose(), 5: lambda: base_step(0, 0), 6: lambda: base_step(1, 0),
-                 7: lambda: base_step(0, 1), 8: lambda: base_step(1, 1)}
-
-        for i in range(NU + 3):
-            if i < NU:
-                stage_a(i)
-                if i % 2 == 1 and i // 2 + W_BUFS < E:
-                    load_w(i // 2 + W_BUFS, pieces_of(i // 2 + W_BUFS))
-            if i in extra:
-                extra[i]()
-            if 1 <= i <= NU:
-                stage_b(i - 1)
-            if 2 <= i <= NU + 1:
-                stage_c(i - 2)
-            if i >= 3:
-                stage_d(i - 3)
-                if i - 3 >= NU - 2:
-                    finish(i - 3 - (NU - 2))
+        next_load = W_BUFS
+        for s in range(len(bunches) + 1):
+            cur = bunches[s] if s < len(bunches) else []
+            prev = bunches[s - 1] if s > 0 else []
+            for i in cur:
+                transposes(i)
+                if next_load < nu:
+                    load_w(next_load)
+                    next_load += 1
+            side_tensor(s)
+            if s == 0:
+                z_and_gate()
+            if cur:
+                quantise(cur[0])
+            side_vector(s)
+            for i in prev:
+                multiply(i)
+            for i in prev:
+                mix(i)
+                if i in finish_after:
+                    finish(finish_after[i][0], finish_after[i][1])
+            for i in cur[1:]:
+                quantise(i)

@@ -19,7 +19,7 @@ E = 16
 B = 128
 FLOPS = 2 * E * M * M * B + 4 * E * M * B
 
-PIN = False
+PIN = True
 W_BUFS = 12
 TP_BUFS = 6
 V_PERIOD = 4

@@ -22,6 +22,11 @@ FLOPS = 2 * E * M * M * B + 4 * E * M * B
 PIN = True
 W_BUFS = 12
 TP_BUFS = 6
+LAG_M = 3
+LAG_S = 3
+PRE_WARM = 5
+WARM_UNITS = 4
+WARM_BANKS = (0, 1, 3)
 V_PERIOD = 4
 
 
@@ -38,13 +43,12 @@ def tile_dynamix_pb_kernel(tc, z, mlp_out, t2, A, W, h, out):
     nc = tc.nc
     units = make_units()
     nu = len(units)
-    bunches = [[2 * s, 2 * s + 1] for s in range(15)] + [[30, 31, 32]]
     finish_after = {29: (0, 4), 31: (4, 2), 32: (6, 2)}
     with ExitStack() as ctx:
         const = ctx.enter_context(tc.tile_pool(name="const", bufs=1))
         wpool = ctx.enter_context(tc.tile_pool(name="wpool", bufs=W_BUFS))
         gpool = ctx.enter_context(tc.tile_pool(name="gpool", bufs=3))
-        qpool = ctx.enter_context(tc.tile_pool(name="qpool", bufs=3))
+        qpool = ctx.enter_context(tc.tile_pool(name="qpool", bufs=4))
         opool = ctx.enter_context(tc.tile_pool(name="opool", bufs=2))
         pt = ctx.enter_context(tc.psum_pool(name="pt", bufs=TP_BUFS))
         pm = ctx.enter_context(tc.psum_pool(name="pm", bufs=8 - TP_BUFS))
@@ -66,6 +70,8 @@ def tile_dynamix_pb_kernel(tc, z, mlp_out, t2, A, W, h, out):
 
         warm = const.tile([P, 1], F32, name="warm")
         nc.vector.memset(warm[:], 0.0)
+        dz = const.tile([P, 512], BF16, name="dz")
+        nc.vector.memset(dz[:].bitcast(I32), 0)
         ah = const.tile([P, 2 * M], BF16, name="ah")
         nc.vector.memset(ah[:].bitcast(I32), 0)
         xs = const.tile([P, P], BF16, name="xs")
@@ -92,6 +98,14 @@ def tile_dynamix_pb_kernel(tc, z, mlp_out, t2, A, W, h, out):
         nc.sync.dma_start(out=zm[:], in_=z.rearrange("(p t) b -> p (t b)", t=8))
         for i in range(4, W_BUFS):
             load_w(i)
+
+        dps = pm.tile([P, 512], F32, name="dps", tag="ps")
+
+        def dummy():
+            nc.tensor.matmul(dps[:], lhsT=dz[:, 0:P], rhs=dz[:], start=True, stop=True)
+
+        for c in range(PRE_WARM):
+            dummy()
 
         ident_f = const.tile([P, P], F32, name="ident_f")
         make_identity(nc, ident_f[:])
@@ -155,7 +169,7 @@ def tile_dynamix_pb_kernel(tc, z, mlp_out, t2, A, W, h, out):
         side = {}
 
         def side_tensor(s):
-            if s == 2:
+            if s == 4:
                 xp = pt.tile([P, P], BF16, name="xp", tag="tp")
                 nc.tensor.transpose(xp[:], xs[:], ident_b[:])
                 side["xp"] = xp
@@ -163,25 +177,28 @@ def tile_dynamix_pb_kernel(tc, z, mlp_out, t2, A, W, h, out):
                 for t in range(8):
                     nc.tensor.transpose(zp[:, t * P:(t + 1) * P], zm[:, t * P:(t + 1) * P], ident_b[:])
                 nc.scalar.copy(out=zt[:], in_=zp[:])
-            if s in (3, 4):
-                hb = s - 3
-                for a in range(2):
-                    gb = pt.tile([P, 512], F32, name="gb", tag="tp")
-                    col = (a * 8 + 4 * hb) * P
-                    nc.tensor.matmul(gb[:], lhsT=rw[:], rhs=aht[:, col:col + 512], start=True, stop=True)
-                    side[a] = gb
+            if 6 <= s <= 9:
+                hb, a = divmod(s - 6, 2)
+                gb = pt.tile([P, 512], F32, name="gb", tag="tp")
+                col = (a * 8 + 4 * hb) * P
+                nc.tensor.matmul(gb[:], lhsT=rw[:], rhs=aht[:, col:col + 512], start=True, stop=True)
+                side["gb"] = gb
 
         def side_vector(s):
-            if s == 1:
-                gate_split()
             if s == 2:
+                gate_split()
+            if s == 4:
                 nc.vector.tensor_copy(out=rw[:], in_=side["xp"][:])
-            if s in (3, 4):
-                sl = slice((s - 3) * 512, (s - 2) * 512)
-                tmp = opool.tile([P, 512], F32, name="tmp", tag="tmp")
-                nc.vector.tensor_tensor(out=tmp[:], in0=side[0][:], in1=zt[:, sl], op=ALU.mult)
-                nc.vector.tensor_tensor(out=acc[:, sl], in0=side[1][:], in1=acc[:, sl], op=ALU.add)
-                nc.vector.tensor_tensor(out=acc[:, sl], in0=acc[:, sl], in1=tmp[:], op=ALU.add)
+            if 6 <= s <= 9:
+                hb, a = divmod(s - 6, 2)
+                sl = slice(hb * 512, (hb + 1) * 512)
+                if a == 0:
+                    tmp = opool.tile([P, 512], F32, name="tmp", tag="tmp")
+                    nc.vector.tensor_tensor(out=tmp[:], in0=side["gb"][:], in1=zt[:, sl], op=ALU.mult)
+                    side["tmp"] = tmp
+                else:
+                    nc.vector.tensor_tensor(out=side["tmp"][:], in0=side["gb"][:], in1=side["tmp"][:], op=ALU.add)
+                    nc.vector.tensor_tensor(out=acc[:, sl], in0=acc[:, sl], in1=side["tmp"][:], op=ALU.add)
 
         g_tiles = {}
         q_tiles = {}
@@ -207,6 +224,8 @@ def tile_dynamix_pb_kernel(tc, z, mlp_out, t2, A, W, h, out):
                         nc.vector.tensor_copy(out=dst, in_=srcv)
                     else:
                         nc.scalar.copy(out=dst, in_=srcv)
+                    if i < WARM_UNITS and 2 * tp + g in WARM_BANKS:
+                        dummy()
                 if i == 0 and tp == 0:
                     gate_exp()
             g_tiles[i] = gt
@@ -224,11 +243,8 @@ def tile_dynamix_pb_kernel(tc, z, mlp_out, t2, A, W, h, out):
             e, t0, nt = units[i]
             cw, cs = q_tiles[i]
             n = nt * P
-            if nt == 2 and t0 % 4 == 2:
-                ps, c0 = m_tiles[i - 1][0], 256
-            else:
-                ps = pm.tile([P, 512], F32, name="ps", tag="ps")
-                c0 = 0
+            ps = pm.tile([P, 512], F32, name="ps", tag="ps")
+            c0 = 0
             for g in range(2):
                 nc.tensor.matmul_mx(
                     out=ps[:, c0:c0 + n],
@@ -267,25 +283,21 @@ def tile_dynamix_pb_kernel(tc, z, mlp_out, t2, A, W, h, out):
             )
 
         next_load = W_BUFS
-        for s in range(len(bunches) + 1):
-            cur = bunches[s] if s < len(bunches) else []
-            prev = bunches[s - 1] if s > 0 else []
-            for i in cur:
-                transposes(i)
+        for s in range(nu + max(LAG_M, LAG_S)):
+            if s < nu:
+                transposes(s)
                 if next_load < nu:
                     load_w(next_load)
                     next_load += 1
             side_tensor(s)
             if s == 0:
                 z_and_gate()
-            if cur:
-                quantise(cur[0])
+            if 1 <= s <= nu:
+                quantise(s - 1)
             side_vector(s)
-            for i in prev:
-                multiply(i)
-            for i in prev:
-                mix(i)
-                if i in finish_after:
-                    finish(finish_after[i][0], finish_after[i][1])
-            for i in cur[1:]:
-                quantise(i)
+            if 0 <= s - LAG_M < nu:
+                multiply(s - LAG_M)
+            if 0 <= s - LAG_S < nu:
+                mix(s - LAG_S)
+                if s - LAG_S in finish_after:
+                    finish(finish_after[s - LAG_S][0], finish_after[s - LAG_S][1])

@@ -27,7 +27,7 @@ LAG_S = 3
 PRE_WARM = 5
 WARM_UNITS = 4
 WARM_BANKS = (0, 1, 3)
-V_PERIOD = 4
+V_PERIOD = 2
 
 
 def make_units():

@@ -27,7 +27,7 @@ LAG_S = 3
 PRE_WARM = 5
 WARM_UNITS = 4
 WARM_BANKS = (0, 1, 3)
-V_PERIOD = 2
+V_PERIOD = 1000
 
 
 def make_units():

@@ -21,13 +21,14 @@ FLOPS = 2 * E * M * M * B + 4 * E * M * B
 
 PIN = True
 W_BUFS = 12
-TP_BUFS = 6
+TP_BUFS = 5
 LAG_M = 3
-LAG_S = 3
-PRE_WARM = 5
-WARM_UNITS = 4
+LAG_S = 4
+PRE_WARM = 7
+WARM_UNITS = 3
 WARM_BANKS = (0, 1, 3)
-V_PERIOD = 1000
+V_LAST = 28
+V_PERIOD = 4
 
 
 def make_units():
@@ -220,7 +221,7 @@ def tile_dynamix_pb_kernel(tc, z, mlp_out, t2, A, W, h, out):
                     off = g * nt * 256 + tp * 512
                     dst = g32[:, off:off + 512].rearrange("p (c u) -> p c u", u=2)
                     srcv = bank[:].rearrange("p (u c) -> p c u", u=2)
-                    if i % V_PERIOD == 0 and i > 0 and nt == 4 and tp == 1 and g == 1:
+                    if i % V_PERIOD == 0 and 0 < i < V_LAST and tp == 1 and g == 1:
                         nc.vector.tensor_copy(out=dst, in_=srcv)
                     else:
                         nc.scalar.copy(out=dst, in_=srcv)
@@ -292,12 +293,12 @@ def tile_dynamix_pb_kernel(tc, z, mlp_out, t2, A, W, h, out):
             side_tensor(s)
             if s == 0:
                 z_and_gate()
-            if 1 <= s <= nu:
-                quantise(s - 1)
-            side_vector(s)
             if 0 <= s - LAG_M < nu:
                 multiply(s - LAG_M)
             if 0 <= s - LAG_S < nu:
                 mix(s - LAG_S)
                 if s - LAG_S in finish_after:
                     finish(finish_after[s - LAG_S][0], finish_after[s - LAG_S][1])
+            if 1 <= s <= nu:
+                quantise(s - 1)
+            side_vector(s)

from contextlib import ExitStack

import concourse.mybir as mybir
from concourse.masks import make_identity

F32 = mybir.dt.float32
BF16 = mybir.dt.bfloat16
I32 = mybir.dt.int32
U32 = mybir.dt.uint32
U8 = mybir.dt.uint8
FP8X4 = mybir.dt.float8_e4m3fn_x4
ALU = mybir.AluOpType
ACT = mybir.ActivationFunctionType
AX = mybir.AxisListType

P = 128
M = 1024
E = 16
B = 128
FLOPS = 2 * E * M * M * B + 4 * E * M * B

PIN = True
W_BUFS = 12
TP_BUFS = 5
LAG_M = 3
LAG_S = 4
PRE_WARM = 7
WARM_UNITS = 3
WARM_BANKS = (0, 1, 3)
V_LAST = 28
V_PERIOD = 4


def make_units():
    units = []
    for e in range(E - 2):
        units.append((e, 0, 4))
        units.append((e, 4, 4))
    units.extend([(E - 2, 0, 4), (E - 1, 0, 4), (E - 2, 4, 4), (E - 1, 4, 2), (E - 1, 6, 2)])
    return units


def tile_dynamix_pb_kernel(tc, z, mlp_out, t2, A, W, h, out):
    nc = tc.nc
    units = make_units()
    nu = len(units)
    finish_after = {29: (0, 4), 31: (4, 2), 32: (6, 2)}
    with ExitStack() as ctx:
        const = ctx.enter_context(tc.tile_pool(name="const", bufs=1))
        wpool = ctx.enter_context(tc.tile_pool(name="wpool", bufs=W_BUFS))
        gpool = ctx.enter_context(tc.tile_pool(name="gpool", bufs=3))
        qpool = ctx.enter_context(tc.tile_pool(name="qpool", bufs=4))
        opool = ctx.enter_context(tc.tile_pool(name="opool", bufs=2))
        pt = ctx.enter_context(tc.psum_pool(name="pt", bufs=TP_BUFS))
        pm = ctx.enter_context(tc.psum_pool(name="pm", bufs=8 - TP_BUFS))
        if PIN:
            ctx.enter_context(tc.manual_schedule())

        w_tiles = {}

        def load_w(i, pieces=1):
            e, t0, nt = units[i]
            wt = wpool.tile([P, 4 * M], BF16, name="wt", tag="wt")
            src = W[e].rearrange("(p t) k -> p (t k)", t=8)
            step = nt * M // pieces
            for c in range(pieces):
                nc.sync.dma_start(
                    out=wt[:, c * step:(c + 1) * step], in_=src[:, t0 * M + c * step:t0 * M + (c + 1) * step]
                )
            w_tiles[i] = wt

        warm = const.tile([P, 1], F32, name="warm")
        nc.vector.memset(warm[:], 0.0)
        dz = const.tile([P, 512], BF16, name="dz")
        nc.vector.memset(dz[:].bitcast(I32), 0)
        ah = const.tile([P, 2 * M], BF16, name="ah")
        nc.vector.memset(ah[:].bitcast(I32), 0)
        xs = const.tile([P, P], BF16, name="xs")
        nc.vector.memset(xs[:].bitcast(I32), 0)
        warm2 = const.tile([P, 1], F32, name="warm2")
        nc.scalar.activation(out=warm2[:], in_=warm[:], func=ACT.Exp)

        mlp = const.tile([P, E], BF16, name="mlp")
        nc.sync.dma_start(out=mlp[:], in_=mlp_out)
        t2b = const.tile([P, 1], BF16, name="t2b")
        nc.sync.dma_start(out=t2b[:], in_=t2.partition_broadcast(P))
        load_w(0, pieces=2)
        zq = const.tile([P, 8 * B], BF16, name="zq")
        nc.sync.dma_start(
            out=zq[:].rearrange("p (c x) -> p c x", c=4),
            in_=z.rearrange("(c p e) b -> p c (e b)", c=4, p=P, e=2),
        )
        for i in range(1, 4):
            load_w(i)
        for s in range(3):
            nc.sync.dma_start(out=ah[16 * s:16 * s + 16, 0:M], in_=A)
            nc.sync.dma_start(out=ah[16 * s:16 * s + 16, M:2 * M], in_=h)
        zm = const.tile([P, 8 * B], BF16, name="zm")
        nc.sync.dma_start(out=zm[:], in_=z.rearrange("(p t) b -> p (t b)", t=8))
        for i in range(4, W_BUFS):
            load_w(i)

        dps = pm.tile([P, 512], F32, name="dps", tag="ps")

        def dummy():
            nc.tensor.matmul(dps[:], lhsT=dz[:, 0:P], rhs=dz[:], start=True, stop=True)

        for c in range(PRE_WARM):
            dummy()

        ident_f = const.tile([P, P], F32, name="ident_f")
        make_identity(nc, ident_f[:])
        ident_b = const.tile([P, P], BF16, name="ident_b")
        make_identity(nc, ident_b[:])
        aht = const.tile([P, 2 * M], BF16, name="aht")
        nc.gpsimd.tensor_scalar(
            out=aht[:].rearrange("k (a t p) -> k a t p", a=2, t=8),
            in0=ah[:].rearrange("k (a p t) -> k a t p", a=2, t=8),
            scalar1=1.0, scalar2=0.0, op0=ALU.mult, op1=ALU.add,
        )

        mask = const.tile([P, 1], F32, name="mask")
        nc.vector.tensor_reduce(out=mask[:], in_=ident_f[:, 112:128], axis=AX.X, op=ALU.add)
        floor = const.tile([P, 1], F32, name="floor")
        nc.vector.tensor_scalar(out=floor[:], in0=mask[:], scalar1=-1.0, scalar2=3.4e38, op0=ALU.add, op1=ALU.mult)

        rt = const.tile([P, 1], F32, name="rt")
        nc.vector.reciprocal(out=rt[:], in_=t2b[:])
        lg = const.tile([P, E], F32, name="lg")
        nc.vector.tensor_scalar(out=lg[:], in0=mlp[:], scalar1=rt[:, 0:1], scalar2=-1.0, op0=ALU.mult, op1=ALU.mult)
        mx = const.tile([P, 1], F32, name="mx")
        nc.vector.tensor_reduce(out=mx[:], in_=lg[:], axis=AX.X, op=ALU.max)
        nmx = const.tile([P, 1], F32, name="nmx")
        nc.vector.tensor_scalar(out=nmx[:], in0=mx[:], scalar1=-1.0, scalar2=None, op0=ALU.mult)
        ex = const.tile([P, E], F32, name="ex")
        sm = const.tile([P, 1], F32, name="sm")
        rs = const.tile([P, 1], F32, name="rs")
        wg = const.tile([P, E], F32, name="wg")
        zg = const.tile([P, 8 * B], BF16, name="zg", align_bytes=64)
        zc = const.tile([P, 2 * B], U32, name="zc", align_bytes=64)
        zs = const.tile([P, 2 * B], U8, name="zs", align_bytes=64)
        acc = const.tile([P, M], F32, name="acc")
        rw = const.tile([P, B], BF16, name="rw")
        zt = const.tile([P, M], BF16, name="zt")

        def gate_exp():
            nc.scalar.activation(out=ex[:], in_=lg[:], func=ACT.Exp, bias=nmx[:, 0:1], scale=1.0, accum_out=sm[:])

        def z_and_gate():
            nc.vector.tensor_scalar(
                out=zq[:, 768:1024], in0=zq[:, 768:1024], scalar1=floor[:, 0:1], scalar2=None, op0=ALU.max
            )
            nc.vector.tensor_copy(
                out=zg[:].rearrange("p (g b j) -> p g b j", g=2, j=4),
                in_=zq[:].rearrange("p (g j b) -> p g b j", g=2, j=4),
            )
            nc.vector.reciprocal(out=rs[:], in_=sm[:])
            nc.vector.tensor_scalar(out=wg[:], in0=ex[:], scalar1=rs[:, 0:1], scalar2=None, op0=ALU.mult)
            nc.vector.quantize_mx(out=zc[:].bitcast(FP8X4), scales=zs[:], in_=zg[:])

        def gate_split():
            nc.vector.tensor_copy(out=xs[:, 0:16], in_=wg[:])
            r1 = const.tile([P, E], F32, name="r1")
            nc.vector.tensor_tensor(out=r1[:], in0=wg[:], in1=xs[:, 0:16], op=ALU.subtract)
            nc.vector.tensor_copy(out=xs[:, 16:32], in_=r1[:])
            r2 = const.tile([P, E], F32, name="r2")
            nc.vector.tensor_tensor(out=r2[:], in0=r1[:], in1=xs[:, 16:32], op=ALU.subtract)
            nc.vector.tensor_copy(out=xs[:, 32:48], in_=r2[:])

        side = {}

        def side_tensor(s):
            if s == 4:
                xp = pt.tile([P, P], BF16, name="xp", tag="tp")
                nc.tensor.transpose(xp[:], xs[:], ident_b[:])
                side["xp"] = xp
                zp = pt.tile([P, M], BF16, name="zp", tag="tp")
                for t in range(8):
                    nc.tensor.transpose(zp[:, t * P:(t + 1) * P], zm[:, t * P:(t + 1) * P], ident_b[:])
                nc.scalar.copy(out=zt[:], in_=zp[:])
            if 6 <= s <= 9:
                hb, a = divmod(s - 6, 2)
                gb = pt.tile([P, 512], F32, name="gb", tag="tp")
                col = (a * 8 + 4 * hb) * P
                nc.tensor.matmul(gb[:], lhsT=rw[:], rhs=aht[:, col:col + 512], start=True, stop=True)
                side["gb"] = gb

        def side_vector(s):
            if s == 2:
                gate_split()
            if s == 4:
                nc.vector.tensor_copy(out=rw[:], in_=side["xp"][:])
            if 6 <= s <= 9:
                hb, a = divmod(s - 6, 2)
                sl = slice(hb * 512, (hb + 1) * 512)
                if a == 0:
                    tmp = opool.tile([P, 512], F32, name="tmp", tag="tmp")
                    nc.vector.tensor_tensor(out=tmp[:], in0=side["gb"][:], in1=zt[:, sl], op=ALU.mult)
                    side["tmp"] = tmp
                else:
                    nc.vector.tensor_tensor(out=side["tmp"][:], in0=side["gb"][:], in1=side["tmp"][:], op=ALU.add)
                    nc.vector.tensor_tensor(out=acc[:, sl], in0=acc[:, sl], in1=side["tmp"][:], op=ALU.add)

        g_tiles = {}
        q_tiles = {}
        m_tiles = {}

        def transposes(i):
            e, t0, nt = units[i]
            w32 = w_tiles[i][:].bitcast(F32)
            gt = gpool.tile([P, 4096], BF16, name="gt", tag="gt", align_bytes=64)
            g32 = gt[:].bitcast(F32)
            for tp in range(nt // 2):
                for g in range(2):
                    bank = pt.tile([P, 512], F32, name="bank", tag="tp")
                    for u in range(2):
                        for t_ in range(2):
                            col = (2 * tp + t_) * 512 + (2 * g + u) * P
                            pos = (2 * u + t_) * P
                            nc.tensor.transpose(bank[:, pos:pos + P], w32[:, col:col + P], ident_f[:])
                    off = g * nt * 256 + tp * 512
                    dst = g32[:, off:off + 512].rearrange("p (c u) -> p c u", u=2)
                    srcv = bank[:].rearrange("p (u c) -> p c u", u=2)
                    if i % V_PERIOD == 0 and 0 < i < V_LAST and tp == 1 and g == 1:
                        nc.vector.tensor_copy(out=dst, in_=srcv)
                    else:
                        nc.scalar.copy(out=dst, in_=srcv)
                    if i < WARM_UNITS and 2 * tp + g in WARM_BANKS:
                        dummy()
                if i == 0 and tp == 0:
                    gate_exp()
            g_tiles[i] = gt

        def quantise(i):
            nt = units[i][2]
            cw = qpool.tile([P, 1024], U32, name="cw", tag="cw", align_bytes=64)
            cs = qpool.tile([P, 1024], U8, name="cs", tag="cs", align_bytes=64)
            nc.vector.quantize_mx(
                out=cw[:, 0:nt * 256].bitcast(FP8X4), scales=cs[:, 0:nt * 256], in_=g_tiles[i][:, 0:nt * 1024]
            )
            q_tiles[i] = (cw, cs)

        def multiply(i):
            e, t0, nt = units[i]
            cw, cs = q_tiles[i]
            n = nt * P
            ps = pm.tile([P, 512], F32, name="ps", tag="ps")
            c0 = 0
            for g in range(2):
                nc.tensor.matmul_mx(
                    out=ps[:, c0:c0 + n],
                    lhsT=zc[:, g * B:(g + 1) * B].bitcast(FP8X4),
                    lhsT_scale=zs[:, g * B:(g + 1) * B],
                    rhs=cw[:, g * n:(g + 1) * n].bitcast(FP8X4),
                    rhs_scale=cs[:, g * n:(g + 1) * n],
                    start=(g == 0),
                    stop=(g == 1),
                )
            m_tiles[i] = (ps, c0)

        def mix(i):
            e, t0, nt = units[i]
            ps, c0 = m_tiles[i]
            sl = slice(t0 * P, (t0 + nt) * P)
            if e == 0:
                nc.vector.tensor_scalar(
                    out=acc[:, sl], in0=ps[:, c0:c0 + nt * P], scalar1=wg[:, 0:1], scalar2=None, op0=ALU.mult
                )
            else:
                nc.vector.scalar_tensor_tensor(
                    out=acc[:, sl], in0=ps[:, c0:c0 + nt * P], scalar=wg[:, e:e + 1], in1=acc[:, sl],
                    op0=ALU.mult, op1=ALU.add,
                )

        def finish(t0, nt):
            fb = pt.tile([P, 512], F32, name="fb", tag="tp")
            for tl in range(nt):
                col = (t0 + tl) * P
                nc.tensor.transpose(fb[:, tl * P:(tl + 1) * P], acc[:, col:col + P], ident_f[:])
            fin = opool.tile([P, 512], F32, name="fin", tag="fin")
            nc.scalar.copy(out=fin[:, 0:nt * P], in_=fb[:, 0:nt * P])
            nc.sync.dma_start(
                out=out.rearrange("(p t) b -> p (t b)", t=8)[:, t0 * P:(t0 + nt) * P], in_=fin[:, 0:nt * P]
            )

        next_load = W_BUFS
        for s in range(nu + max(LAG_M, LAG_S)):
            if s < nu:
                transposes(s)
                if next_load < nu:
                    load_w(next_load)
                    next_load += 1
            side_tensor(s)
            if s == 0:
                z_and_gate()
            if 0 <= s - LAG_M < nu:
                multiply(s - LAG_M)
            if 0 <= s - LAG_S < nu:
                mix(s - LAG_S)
                if s - LAG_S in finish_after:
                    finish(finish_after[s - LAG_S][0], finish_after[s - LAG_S][1])
            if 1 <= s <= nu:
                quantise(s - 1)
            side_vector(s)
